import numpy as np
import ml_dtypes

BF16 = ml_dtypes.bfloat16


def bf(x):
    return np.asarray(x, np.float32).astype(BF16)


def f32(x):
    return np.asarray(x, np.float32)


def f64(x):
    return np.asarray(x).astype(np.float64)


def striped(idx):
    return np.tile(idx.reshape(-1, 16).T, (8, 1))


C, HALF, F, S, N = 256, 128, 1024, 1024, 512


def silu(v):
    return v / (1.0 + np.exp(-v))


def setup_inputs():
    return {
        "atom_tab": f32(np.random.standard_normal((C, S))),
        "t": f32(np.random.uniform(0.0, 1.0, (1, N))),
        "tw": f32(np.random.uniform(-0.25, 0.25, (HALF, 1))),
        "w1": bf(1.5 * np.random.standard_normal((C, F)) / np.sqrt(C)),
        "b1": f32(0.1 * np.random.standard_normal((F, 1))),
        "w2": bf(1.5 * np.random.standard_normal((F, C)) / np.sqrt(F)),
        "b2": f32(0.1 * np.random.standard_normal((C, 1))),
        "offs": striped(np.random.permutation(np.tile(np.arange(S), 2))[:N]),
    }


def reference(atom_tab, t, tw, w1, b1, w2, b2, offs):
    idx = offs[:16].T.reshape(-1)
    p = 2.0 * np.pi * f64(tw) * f64(t)
    e = np.concatenate([np.sin(p), np.cos(p)], axis=0)
    u = silu(f64(w1).T @ e + f64(b1))
    te = f64(w2).T @ u + f64(b2)
    return f64(atom_tab)[:, idx] + te

@@ -1,0 +1,76 @@
+import math
+
+import concourse.mybir as mybir
+
+F32 = mybir.dt.float32
+BF16 = mybir.dt.bfloat16
+U16 = mybir.dt.uint16
+FUNC = mybir.ActivationFunctionType
+ADD = mybir.AluOpType.add
+
+P = 128
+C, F, S, N = 256, 1024, 1024, 512
+KB = C // P
+FB = F // P
+CB = C // P
+
+FLOPS = 2 * N * (C * F + F * C)
+
+
+def tile_cdvae_kernel(tc, atom_tab, t, tw, w1, b1, w2, b2, offs, out):
+    nc = tc.nc
+    with (
+        tc.tile_pool(name="held", bufs=1) as held,
+        tc.tile_pool(name="work", bufs=2) as work,
+        tc.psum_pool(name="hidden", bufs=4) as hidden,
+        tc.psum_pool(name="summed", bufs=2) as summed,
+    ):
+        t_all = held.tile([P, N], F32, name="t_all")
+        nc.sync.dma_start(t_all[:], t.to_broadcast([P, N]))
+        tw_col = held.tile([P, 1], F32, name="tw_col")
+        nc.sync.dma_start(tw_col[:], tw)
+        w1_sb = [held.tile([P, F], BF16, name=f"w1_{kb}") for kb in range(KB)]
+        for kb in range(KB):
+            nc.sync.dma_start(w1_sb[kb][:], w1[kb * P : (kb + 1) * P, :])
+        offsets = held.tile([P, N // 16], U16, name="offsets")
+        nc.sync.dma_start(offsets[:], offs)
+        b1_sb = held.tile([P, FB], F32, name="b1_sb")
+        b2_sb = held.tile([P, CB], F32, name="b2_sb")
+        with nc.allow_non_contiguous_dma(reason="a bias: one float32 for each partition and block"):
+            nc.sync.dma_start(b1_sb[:], b1.rearrange("(fb p) one -> p (fb one)", p=P))
+        w2_sb = held.tile([P, FB, C], BF16, name="w2_sb")
+        nc.sync.dma_start(w2_sb[:], w2.rearrange("(fb p) c -> p fb c", p=P))
+        with nc.allow_non_contiguous_dma(reason="a bias: one float32 for each partition and block"):
+            nc.sync.dma_start(b2_sb[:], b2.rearrange("(cb p) one -> p (cb one)", p=P))
+        table = [held.tile([P, S], F32, name=f"table{cb}") for cb in range(CB)]
+        for cb in range(CB):
+            nc.sync.dma_start(table[cb][:], atom_tab[cb * P : (cb + 1) * P, :])
+
+        turn = held.tile([P, 1], F32, name="turn")
+        nc.vector.tensor_scalar_mul(turn[:], tw_col[:], 2.0 * math.pi)
+        quarter = held.tile([P, 1], F32, name="quarter")
+        nc.vector.memset(quarter[:], 0.5 * math.pi)
+        e = [held.tile([P, N], BF16, name=f"e{kb}") for kb in range(KB)]
+        nc.scalar.activation(e[0][:], t_all[:], FUNC.Sin, scale=turn[:])
+        nc.scalar.activation(e[1][:], t_all[:], FUNC.Sin, bias=quarter[:], scale=turn[:])
+
+        u = [held.tile([P, N], BF16, name=f"u{fb}") for fb in range(FB)]
+        for fb in range(FB):
+            v = hidden.tile([P, N], F32, name="v")
+            for kb in range(KB):
+                nc.tensor.matmul(
+                    v[:], w1_sb[kb][:, fb * P : (fb + 1) * P], e[kb][:], start=kb == 0, stop=kb == KB - 1
+                )
+            nc.scalar.activation(u[fb][:], v[:], FUNC.Silu, bias=b1_sb[:, fb : fb + 1])
+
+        for cb in range(CB):
+            acc = summed.tile([P, N], F32, name="acc")
+            for fb in range(FB):
+                nc.tensor.matmul(
+                    acc[:], w2_sb[:, fb, cb * P : (cb + 1) * P], u[fb][:], start=fb == 0, stop=fb == FB - 1
+                )
+            te = work.tile([P, N], F32, name="te")
+            nc.scalar.activation(te[:], acc[:], FUNC.Identity, bias=b2_sb[:, cb : cb + 1])
+            res = work.tile([P, N], F32, name="res")
+            nc.vector.tensor_tensor(res[:], table[cb][:].indirect(offsets[:]), te[:], ADD)
+            nc.sync.dma_start(out[cb * P : (cb + 1) * P, :], res[:])

@@ -25,6 +25,11 @@ def tile_cdvae_kernel(tc, atom_tab, t, tw, w1, b1, w2, b2, offs, out):
         tc.psum_pool(name="hidden", bufs=4) as hidden,
         tc.psum_pool(name="summed", bufs=2) as summed,
     ):
+        zero = held.tile([P, 1], F32, name="zero")
+        nc.vector.memset(zero[:], 0.0)
+        primed = held.tile([P, 1], F32, name="primed")
+        nc.scalar.activation(primed[:], zero[:], FUNC.Silu)
+
         t_all = held.tile([P, N], F32, name="t_all")
         nc.sync.dma_start(t_all[:], t.to_broadcast([P, N]))
         tw_col = held.tile([P, 1], F32, name="tw_col")

@@ -30,6 +30,12 @@ def tile_cdvae_kernel(tc, atom_tab, t, tw, w1, b1, w2, b2, offs, out):
         primed = held.tile([P, 1], F32, name="primed")
         nc.scalar.activation(primed[:], zero[:], FUNC.Silu)
 
+        idle = held.tile([P, N], BF16, name="idle")
+        nc.vector.memset(idle[:], 0.0)
+        spin = hidden.tile([P, N], F32, name="spin", bufs=1)
+        for rep in range(4):
+            nc.tensor.matmul(spin[:], idle[:, 0:P], idle[:], start=True, stop=True)
+
         t_all = held.tile([P, N], F32, name="t_all")
         nc.sync.dma_start(t_all[:], t.to_broadcast([P, N]))
         tw_col = held.tile([P, 1], F32, name="tw_col")

@@ -13,6 +13,7 @@ C, F, S, N = 256, 1024, 1024, 512
 KB = C // P
 FB = F // P
 CB = C // P
+GROUP = 4
 
 FLOPS = 2 * N * (C * F + F * C)
 
@@ -22,7 +23,7 @@ def tile_cdvae_kernel(tc, atom_tab, t, tw, w1, b1, w2, b2, offs, out):
     with (
         tc.tile_pool(name="held", bufs=1) as held,
         tc.tile_pool(name="work", bufs=2) as work,
-        tc.psum_pool(name="hidden", bufs=4) as hidden,
+        tc.psum_pool(name="hidden", bufs=5) as hidden,
         tc.psum_pool(name="summed", bufs=2) as summed,
     ):
         zero = held.tile([P, 1], F32, name="zero")
@@ -36,23 +37,22 @@ def tile_cdvae_kernel(tc, atom_tab, t, tw, w1, b1, w2, b2, offs, out):
         for rep in range(4):
             nc.tensor.matmul(spin[:], idle[:, 0:P], idle[:], start=True, stop=True)
 
+        tw_col = held.tile([P, 1], F32, name="tw_col")
+        nc.scalar.dma_start(tw_col[:], tw)
         t_all = held.tile([P, N], F32, name="t_all")
         nc.sync.dma_start(t_all[:], t.to_broadcast([P, N]))
-        tw_col = held.tile([P, 1], F32, name="tw_col")
-        nc.sync.dma_start(tw_col[:], tw)
         w1_sb = [held.tile([P, F], BF16, name=f"w1_{kb}") for kb in range(KB)]
         for kb in range(KB):
             nc.sync.dma_start(w1_sb[kb][:], w1[kb * P : (kb + 1) * P, :])
         offsets = held.tile([P, N // 16], U16, name="offsets")
         nc.sync.dma_start(offsets[:], offs)
         b1_sb = held.tile([P, FB], F32, name="b1_sb")
-        b2_sb = held.tile([P, CB], F32, name="b2_sb")
-        with nc.allow_non_contiguous_dma(reason="a bias: one float32 for each partition and block"):
-            nc.sync.dma_start(b1_sb[:], b1.rearrange("(fb p) one -> p (fb one)", p=P))
+        nc.sync.dma_start(b1_sb[:], b1.rearrange("(p fb) one -> p (fb one)", fb=FB))
         w2_sb = held.tile([P, FB, C], BF16, name="w2_sb")
-        nc.sync.dma_start(w2_sb[:], w2.rearrange("(fb p) c -> p fb c", p=P))
-        with nc.allow_non_contiguous_dma(reason="a bias: one float32 for each partition and block"):
-            nc.sync.dma_start(b2_sb[:], b2.rearrange("(cb p) one -> p (cb one)", p=P))
+        nc.sync.dma_start(w2_sb[:], w2.rearrange("(p fb) c -> p fb c", fb=FB))
+        b2_sb = held.tile([P, CB], F32, name="b2_sb")
+        with nc.allow_non_contiguous_dma(reason="b2: one float32 for each partition and channel block"):
+            nc.gpsimd.dma_start(b2_sb[:], b2.rearrange("(cb p) one -> p (cb one)", p=P))
         table = [held.tile([P, S], F32, name=f"table{cb}") for cb in range(CB)]
         for cb in range(CB):
             nc.sync.dma_start(table[cb][:], atom_tab[cb * P : (cb + 1) * P, :])
@@ -66,13 +66,17 @@ def tile_cdvae_kernel(tc, atom_tab, t, tw, w1, b1, w2, b2, offs, out):
         nc.scalar.activation(e[1][:], t_all[:], FUNC.Sin, bias=quarter[:], scale=turn[:])
 
         u = [held.tile([P, N], BF16, name=f"u{fb}") for fb in range(FB)]
-        for fb in range(FB):
-            v = hidden.tile([P, N], F32, name="v")
+        w1_blocks = [w1_sb[kb][:].rearrange("k (p fb) -> k fb p", fb=FB) for kb in range(KB)]
+        for first in range(0, FB, GROUP):
+            group = range(first, first + GROUP)
+            v = {fb: hidden.tile([P, N], F32, name="v") for fb in group}
             for kb in range(KB):
-                nc.tensor.matmul(
-                    v[:], w1_sb[kb][:, fb * P : (fb + 1) * P], e[kb][:], start=kb == 0, stop=kb == KB - 1
-                )
-            nc.scalar.activation(u[fb][:], v[:], FUNC.Silu, bias=b1_sb[:, fb : fb + 1])
+                for fb in group:
+                    nc.tensor.matmul(
+                        v[fb][:], w1_blocks[kb][:, fb, :], e[kb][:], start=kb == 0, stop=kb == KB - 1
+                    )
+            for fb in group:
+                nc.scalar.activation(u[fb][:], v[fb][:], FUNC.Silu, bias=b1_sb[:, fb : fb + 1])
 
         for cb in range(CB):
             acc = summed.tile([P, N], F32, name="acc")

@@ -13,7 +13,8 @@ C, F, S, N = 256, 1024, 1024, 512
 KB = C // P
 FB = F // P
 CB = C // P
-GROUP = 4
+PIECE = 128
+GROUP = 2
 
 FLOPS = 2 * N * (C * F + F * C)
 
@@ -22,9 +23,8 @@ def tile_cdvae_kernel(tc, atom_tab, t, tw, w1, b1, w2, b2, offs, out):
     nc = tc.nc
     with (
         tc.tile_pool(name="held", bufs=1) as held,
-        tc.tile_pool(name="work", bufs=2) as work,
-        tc.psum_pool(name="hidden", bufs=5) as hidden,
-        tc.psum_pool(name="summed", bufs=2) as summed,
+        tc.psum_pool(name="hidden", bufs=4) as hidden,
+        tc.psum_pool(name="summed", bufs=4) as summed,
     ):
         zero = held.tile([P, 1], F32, name="zero")
         nc.vector.memset(zero[:], 0.0)
@@ -33,7 +33,7 @@ def tile_cdvae_kernel(tc, atom_tab, t, tw, w1, b1, w2, b2, offs, out):
 
         idle = held.tile([P, N], BF16, name="idle")
         nc.vector.memset(idle[:], 0.0)
-        spin = hidden.tile([P, N], F32, name="spin", bufs=1)
+        spin = summed.tile([P, N], F32, name="spin", tag="acc")
         for rep in range(4):
             nc.tensor.matmul(spin[:], idle[:, 0:P], idle[:], start=True, stop=True)
 
@@ -79,13 +79,16 @@ def tile_cdvae_kernel(tc, atom_tab, t, tw, w1, b1, w2, b2, offs, out):
                 nc.scalar.activation(u[fb][:], v[fb][:], FUNC.Silu, bias=b1_sb[:, fb : fb + 1])
 
         for cb in range(CB):
-            acc = summed.tile([P, N], F32, name="acc")
-            for fb in range(FB):
-                nc.tensor.matmul(
-                    acc[:], w2_sb[:, fb, cb * P : (cb + 1) * P], u[fb][:], start=fb == 0, stop=fb == FB - 1
-                )
-            te = work.tile([P, N], F32, name="te")
-            nc.scalar.activation(te[:], acc[:], FUNC.Identity, bias=b2_sb[:, cb : cb + 1])
-            res = work.tile([P, N], F32, name="res")
-            nc.vector.tensor_tensor(res[:], table[cb][:].indirect(offsets[:]), te[:], ADD)
-            nc.sync.dma_start(out[cb * P : (cb + 1) * P, :], res[:])
+            te = held.tile([P, N], F32, name=f"te{cb}")
+            res = held.tile([P, N], F32, name=f"res{cb}")
+            for first in range(0, N, PIECE):
+                piece = slice(first, first + PIECE)
+                acc = summed.tile([P, PIECE], F32, name="acc")
+                for fb in range(FB):
+                    nc.tensor.matmul(
+                        acc[:], w2_sb[:, fb, cb * P : (cb + 1) * P], u[fb][:, piece], start=fb == 0, stop=fb == FB - 1
+                    )
+                nc.scalar.activation(te[:, piece], acc[:], FUNC.Identity, bias=b2_sb[:, cb : cb + 1])
+                picked = table[cb][:].indirect(offsets[:, first // 16 : (first + PIECE) // 16])
+                nc.vector.tensor_tensor(res[:, piece], picked, te[:, piece], ADD)
+                nc.sync.dma_start(out[cb * P : (cb + 1) * P, piece], res[:, piece])

@@ -14,7 +14,10 @@ KB = C // P
 FB = F // P
 CB = C // P
 PIECE = 128
-GROUP = 2
+SMALL = 64
+HALF = N // 2
+GROUP = 4
+GB = FB // GROUP
 
 FLOPS = 2 * N * (C * F + F * C)
 
@@ -23,72 +26,93 @@ def tile_cdvae_kernel(tc, atom_tab, t, tw, w1, b1, w2, b2, offs, out):
     nc = tc.nc
     with (
         tc.tile_pool(name="held", bufs=1) as held,
-        tc.psum_pool(name="hidden", bufs=4) as hidden,
-        tc.psum_pool(name="summed", bufs=4) as summed,
+        tc.psum_pool(name="banks", bufs=8) as banks,
     ):
+        idle = held.tile([P, N], BF16, name="idle")
+        nc.gpsimd.memset(idle[:], 0.0)
+        spin = banks.tile([P, N], F32, name="spin", tag="bank")
+        for rep in range(4):
+            nc.tensor.matmul(spin[:], idle[:, 0:P], idle[:], start=True, stop=True)
+
+        halves = [slice(first, first + HALF) for first in range(0, N, HALF)]
+
+        tw_col = held.tile([P, 1], F32, name="tw_col")
+        nc.scalar.dma_start(tw_col[:], tw)
+        b1_sb = held.tile([P, GB, GROUP], F32, name="b1_sb")
+        with nc.allow_non_contiguous_dma(reason="b1: GROUP float32 for each partition and group"):
+            nc.scalar.dma_start(b1_sb[:], b1.rearrange("(g p r) one -> p g (r one)", g=GB, r=GROUP))
+        t_all = held.tile([P, N], F32, name="t_all")
+        w1_sb = [[held.tile([P, GROUP * P], BF16, name=f"w1_{kb}_{g}") for g in range(GB)] for kb in range(KB)]
+        nc.sync.dma_start(t_all[:, halves[0]], t[:, halves[0]].to_broadcast([P, HALF]))
+        for g in range(GB):
+            for kb in range(KB):
+                nc.sync.dma_start(w1_sb[kb][g][:], w1[kb * P : (kb + 1) * P, g * GROUP * P : (g + 1) * GROUP * P])
+            if g == 0:
+                nc.sync.dma_start(t_all[:, halves[1]], t[:, halves[1]].to_broadcast([P, HALF]))
+        offsets = held.tile([P, N // 16], U16, name="offsets")
+        nc.sync.dma_start(offsets[:], offs)
+        w2_sb = held.tile([P, GB, GROUP, C], BF16, name="w2_sb")
+        nc.sync.dma_start(w2_sb[:], w2.rearrange("(g p r) c -> p g r c", g=GB, r=GROUP))
+        b2_sb = held.tile([P, CB], F32, name="b2_sb")
+        with nc.allow_non_contiguous_dma(reason="b2: one float32 for each partition and channel block"):
+            nc.scalar.dma_start(b2_sb[:], b2.rearrange("(cb p) one -> p (cb one)", p=P))
+        table = [held.tile([P, S], F32, name=f"table{cb}") for cb in range(CB)]
+        for cb in range(CB):
+            nc.sync.dma_start(table[cb][:], atom_tab[cb * P : (cb + 1) * P, :])
+
         zero = held.tile([P, 1], F32, name="zero")
         nc.vector.memset(zero[:], 0.0)
         primed = held.tile([P, 1], F32, name="primed")
         nc.scalar.activation(primed[:], zero[:], FUNC.Silu)
-
-        idle = held.tile([P, N], BF16, name="idle")
-        nc.vector.memset(idle[:], 0.0)
-        spin = summed.tile([P, N], F32, name="spin", tag="acc")
-        for rep in range(4):
-            nc.tensor.matmul(spin[:], idle[:, 0:P], idle[:], start=True, stop=True)
-
-        tw_col = held.tile([P, 1], F32, name="tw_col")
-        nc.scalar.dma_start(tw_col[:], tw)
-        t_all = held.tile([P, N], F32, name="t_all")
-        nc.sync.dma_start(t_all[:], t.to_broadcast([P, N]))
-        w1_sb = [held.tile([P, F], BF16, name=f"w1_{kb}") for kb in range(KB)]
-        for kb in range(KB):
-            nc.sync.dma_start(w1_sb[kb][:], w1[kb * P : (kb + 1) * P, :])
-        offsets = held.tile([P, N // 16], U16, name="offsets")
-        nc.sync.dma_start(offsets[:], offs)
-        b1_sb = held.tile([P, FB], F32, name="b1_sb")
-        nc.sync.dma_start(b1_sb[:], b1.rearrange("(p fb) one -> p (fb one)", fb=FB))
-        w2_sb = held.tile([P, FB, C], BF16, name="w2_sb")
-        nc.sync.dma_start(w2_sb[:], w2.rearrange("(p fb) c -> p fb c", fb=FB))
-        b2_sb = held.tile([P, CB], F32, name="b2_sb")
-        with nc.allow_non_contiguous_dma(reason="b2: one float32 for each partition and channel block"):
-            nc.gpsimd.dma_start(b2_sb[:], b2.rearrange("(cb p) one -> p (cb one)", p=P))
-        table = [held.tile([P, S], F32, name=f"table{cb}") for cb in range(CB)]
-        for cb in range(CB):
-            nc.sync.dma_start(table[cb][:], atom_tab[cb * P : (cb + 1) * P, :])
 
         turn = held.tile([P, 1], F32, name="turn")
         nc.vector.tensor_scalar_mul(turn[:], tw_col[:], 2.0 * math.pi)
         quarter = held.tile([P, 1], F32, name="quarter")
         nc.vector.memset(quarter[:], 0.5 * math.pi)
         e = [held.tile([P, N], BF16, name=f"e{kb}") for kb in range(KB)]
-        nc.scalar.activation(e[0][:], t_all[:], FUNC.Sin, scale=turn[:])
-        nc.scalar.activation(e[1][:], t_all[:], FUNC.Sin, bias=quarter[:], scale=turn[:])
+        for half in halves:
+            nc.scalar.activation(e[0][:, half], t_all[:, half], FUNC.Sin, scale=turn[:])
+            nc.scalar.activation(e[1][:, half], t_all[:, half], FUNC.Sin, bias=quarter[:], scale=turn[:])
 
-        u = [held.tile([P, N], BF16, name=f"u{fb}") for fb in range(FB)]
-        w1_blocks = [w1_sb[kb][:].rearrange("k (p fb) -> k fb p", fb=FB) for kb in range(KB)]
-        for first in range(0, FB, GROUP):
-            group = range(first, first + GROUP)
-            v = {fb: hidden.tile([P, N], F32, name="v") for fb in group}
-            for kb in range(KB):
-                for fb in group:
-                    nc.tensor.matmul(
-                        v[fb][:], w1_blocks[kb][:, fb, :], e[kb][:], start=kb == 0, stop=kb == KB - 1
-                    )
-            for fb in group:
-                nc.scalar.activation(u[fb][:], v[fb][:], FUNC.Silu, bias=b1_sb[:, fb : fb + 1])
+        u = [[held.tile([P, N], BF16, name=f"u{g}_{r}") for r in range(GROUP)] for g in range(GB)]
+        w1_blocks = [[w1_sb[kb][g][:].rearrange("k (p r) -> k r p", r=GROUP) for g in range(GB)] for kb in range(KB)]
+        for half in halves:
+            for g in range(GB):
+                v = [banks.tile([P, HALF], F32, name="v", tag="bank") for r in range(GROUP)]
+                for kb in range(KB):
+                    for r in range(GROUP):
+                        nc.tensor.matmul(
+                            v[r][:], w1_blocks[kb][g][:, r, :], e[kb][:, half], start=kb == 0, stop=kb == KB - 1
+                        )
+                for r in range(GROUP):
+                    nc.scalar.activation(u[g][r][:, half], v[r][:], FUNC.Silu, bias=b1_sb[:, g, r : r + 1])
 
-        for cb in range(CB):
-            te = held.tile([P, N], F32, name=f"te{cb}")
-            res = held.tile([P, N], F32, name=f"res{cb}")
-            for first in range(0, N, PIECE):
-                piece = slice(first, first + PIECE)
-                acc = summed.tile([P, PIECE], F32, name="acc")
-                for fb in range(FB):
-                    nc.tensor.matmul(
-                        acc[:], w2_sb[:, fb, cb * P : (cb + 1) * P], u[fb][:, piece], start=fb == 0, stop=fb == FB - 1
-                    )
-                nc.scalar.activation(te[:, piece], acc[:], FUNC.Identity, bias=b2_sb[:, cb : cb + 1])
-                picked = table[cb][:].indirect(offsets[:, first // 16 : (first + PIECE) // 16])
-                nc.vector.tensor_tensor(res[:, piece], picked, te[:, piece], ADD)
-                nc.sync.dma_start(out[cb * P : (cb + 1) * P, piece], res[:, piece])
+        te = [held.tile([P, N], F32, name=f"te{cb}") for cb in range(CB)]
+        res = [held.tile([P, N], F32, name=f"res{cb}") for cb in range(CB)]
+        for half in halves:
+            for cb in range(CB):
+                last = half == halves[-1] and cb == CB - 1
+                width = SMALL if last else HALF
+                step = SMALL if last else PIECE
+                for start in range(half.start, half.stop, width):
+                    acc = banks.tile([P, width], F32, name="acc", tag="bank")
+                    for fb in range(FB):
+                        g, r = divmod(fb, GROUP)
+                        nc.tensor.matmul(
+                            acc[:],
+                            w2_sb[:, g, r, cb * P : (cb + 1) * P],
+                            u[g][r][:, start : start + width],
+                            start=fb == 0,
+                            stop=fb == FB - 1,
+                        )
+                    for first in range(start, start + width, step):
+                        piece = slice(first, first + step)
+                        nc.scalar.activation(
+                            te[cb][:, piece],
+                            acc[:, first - start : first - start + step],
+                            FUNC.Identity,
+                            bias=b2_sb[:, cb : cb + 1],
+                        )
+                        picked = table[cb][:].indirect(offsets[:, first // 16 : (first + step) // 16])
+                        nc.vector.tensor_tensor(res[cb][:, piece], picked, te[cb][:, piece], ADD)
+                        nc.sync.dma_start(out[cb * P : (cb + 1) * P, piece], res[cb][:, piece])

@@ -92,27 +92,16 @@ def tile_cdvae_kernel(tc, atom_tab, t, tw, w1, b1, w2, b2, offs, out):
         for half in halves:
             for cb in range(CB):
                 last = half == halves[-1] and cb == CB - 1
-                width = SMALL if last else HALF
                 step = SMALL if last else PIECE
-                for start in range(half.start, half.stop, width):
-                    acc = banks.tile([P, width], F32, name="acc", tag="bank")
+                for first in range(half.start, half.stop, step):
+                    piece = slice(first, first + step)
+                    acc = banks.tile([P, step], F32, name="acc", tag="bank")
                     for fb in range(FB):
                         g, r = divmod(fb, GROUP)
                         nc.tensor.matmul(
-                            acc[:],
-                            w2_sb[:, g, r, cb * P : (cb + 1) * P],
-                            u[g][r][:, start : start + width],
-                            start=fb == 0,
-                            stop=fb == FB - 1,
+                            acc[:], w2_sb[:, g, r, cb * P : (cb + 1) * P], u[g][r][:, piece], start=fb == 0, stop=fb == FB - 1
                         )
-                    for first in range(start, start + width, step):
-                        piece = slice(first, first + step)
-                        nc.scalar.activation(
-                            te[cb][:, piece],
-                            acc[:, first - start : first - start + step],
-                            FUNC.Identity,
-                            bias=b2_sb[:, cb : cb + 1],
-                        )
-                        picked = table[cb][:].indirect(offsets[:, first // 16 : (first + step) // 16])
-                        nc.vector.tensor_tensor(res[cb][:, piece], picked, te[cb][:, piece], ADD)
-                        nc.sync.dma_start(out[cb * P : (cb + 1) * P, piece], res[cb][:, piece])
+                    nc.scalar.activation(te[cb][:, piece], acc[:], FUNC.Identity, bias=b2_sb[:, cb : cb + 1])
+                    picked = table[cb][:].indirect(offsets[:, first // 16 : (first + step) // 16])
+                    nc.vector.tensor_tensor(res[cb][:, piece], picked, te[cb][:, piece], ADD)
+                    nc.sync.dma_start(out[cb * P : (cb + 1) * P, piece], res[cb][:, piece])

@@ -18,6 +18,7 @@ SMALL = 64
 HALF = N // 2
 GROUP = 4
 GB = FB // GROUP
+WARM = 12
 
 FLOPS = 2 * N * (C * F + F * C)
 
@@ -28,27 +29,28 @@ def tile_cdvae_kernel(tc, atom_tab, t, tw, w1, b1, w2, b2, offs, out):
         tc.tile_pool(name="held", bufs=1) as held,
         tc.psum_pool(name="banks", bufs=8) as banks,
     ):
-        idle = held.tile([P, N], BF16, name="idle")
+        idle = held.tile([P, P], BF16, name="idle")
+        tw_pad = held.tile([P, P], F32, name="tw_pad")
+        nc.gpsimd.memset(tw_pad[:], 0.0)
         nc.gpsimd.memset(idle[:], 0.0)
-        spin = banks.tile([P, N], F32, name="spin", tag="bank")
-        for rep in range(4):
-            nc.tensor.matmul(spin[:], idle[:, 0:P], idle[:], start=True, stop=True)
+        spin = banks.tile([P, P], F32, name="spin", tag="bank")
+        for rep in range(WARM):
+            nc.tensor.matmul(spin[:], idle[:], idle[:], start=True, stop=True)
 
         halves = [slice(first, first + HALF) for first in range(0, N, HALF)]
 
-        tw_col = held.tile([P, 1], F32, name="tw_col")
-        nc.scalar.dma_start(tw_col[:], tw)
+        nc.scalar.dma_start(tw_pad[0:1, :], tw.rearrange("k one -> one k"))
         b1_sb = held.tile([P, GB, GROUP], F32, name="b1_sb")
         with nc.allow_non_contiguous_dma(reason="b1: GROUP float32 for each partition and group"):
             nc.scalar.dma_start(b1_sb[:], b1.rearrange("(g p r) one -> p g (r one)", g=GB, r=GROUP))
-        t_all = held.tile([P, N], F32, name="t_all")
+        t_pad = [held.tile([P, HALF], F32, name=f"t_pad{h}") for h in range(len(halves))]
+        for h, half in enumerate(halves):
+            nc.vector.memset(t_pad[h][:], 0.0)
+            nc.sync.dma_start(t_pad[h][0:1, :], t[:, half])
         w1_sb = [[held.tile([P, GROUP * P], BF16, name=f"w1_{kb}_{g}") for g in range(GB)] for kb in range(KB)]
-        nc.sync.dma_start(t_all[:, halves[0]], t[:, halves[0]].to_broadcast([P, HALF]))
         for g in range(GB):
             for kb in range(KB):
                 nc.sync.dma_start(w1_sb[kb][g][:], w1[kb * P : (kb + 1) * P, g * GROUP * P : (g + 1) * GROUP * P])
-            if g == 0:
-                nc.sync.dma_start(t_all[:, halves[1]], t[:, halves[1]].to_broadcast([P, HALF]))
         offsets = held.tile([P, N // 16], U16, name="offsets")
         nc.sync.dma_start(offsets[:], offs)
         w2_sb = held.tile([P, GB, GROUP, C], BF16, name="w2_sb")
@@ -65,14 +67,15 @@ def tile_cdvae_kernel(tc, atom_tab, t, tw, w1, b1, w2, b2, offs, out):
         primed = held.tile([P, 1], F32, name="primed")
         nc.scalar.activation(primed[:], zero[:], FUNC.Silu)
 
-        turn = held.tile([P, 1], F32, name="turn")
-        nc.vector.tensor_scalar_mul(turn[:], tw_col[:], 2.0 * math.pi)
         quarter = held.tile([P, 1], F32, name="quarter")
         nc.vector.memset(quarter[:], 0.5 * math.pi)
         e = [held.tile([P, N], BF16, name=f"e{kb}") for kb in range(KB)]
-        for half in halves:
-            nc.scalar.activation(e[0][:, half], t_all[:, half], FUNC.Sin, scale=turn[:])
-            nc.scalar.activation(e[1][:, half], t_all[:, half], FUNC.Sin, bias=quarter[:], scale=turn[:])
+        turns = [banks.tile([P, HALF], F32, name="turns", tag="bank") for half in halves]
+        for h in range(len(halves)):
+            nc.tensor.matmul(turns[h][:], tw_pad[:], t_pad[h][:], start=True, stop=True)
+        for half, turns_half in zip(halves, turns):
+            nc.scalar.activation(e[0][:, half], turns_half[:], FUNC.Sin, scale=2.0 * math.pi)
+            nc.scalar.activation(e[1][:, half], turns_half[:], FUNC.Sin, bias=quarter[:], scale=2.0 * math.pi)
 
         u = [[held.tile([P, N], BF16, name=f"u{g}_{r}") for r in range(GROUP)] for g in range(GB)]
         w1_blocks = [[w1_sb[kb][g][:].rearrange("k (p r) -> k r p", r=GROUP) for g in range(GB)] for kb in range(KB)]

@@ -39,25 +39,26 @@ def tile_cdvae_kernel(tc, atom_tab, t, tw, w1, b1, w2, b2, offs, out):
 
         halves = [slice(first, first + HALF) for first in range(0, N, HALF)]
 
-        nc.scalar.dma_start(tw_pad[0:1, :], tw.rearrange("k one -> one k"))
-        b1_sb = held.tile([P, GB, GROUP], F32, name="b1_sb")
-        with nc.allow_non_contiguous_dma(reason="b1: GROUP float32 for each partition and group"):
-            nc.scalar.dma_start(b1_sb[:], b1.rearrange("(g p r) one -> p g (r one)", g=GB, r=GROUP))
+        nc.sync.dma_start(tw_pad[0:1, :], tw.rearrange("k one -> one k"))
         t_pad = [held.tile([P, HALF], F32, name=f"t_pad{h}") for h in range(len(halves))]
         for h, half in enumerate(halves):
             nc.vector.memset(t_pad[h][:], 0.0)
             nc.sync.dma_start(t_pad[h][0:1, :], t[:, half])
         w1_sb = [[held.tile([P, GROUP * P], BF16, name=f"w1_{kb}_{g}") for g in range(GB)] for kb in range(KB)]
+        b1_sb = held.tile([P, GB, GROUP], F32, name="b1_sb")
         for g in range(GB):
             for kb in range(KB):
                 nc.sync.dma_start(w1_sb[kb][g][:], w1[kb * P : (kb + 1) * P, g * GROUP * P : (g + 1) * GROUP * P])
-        offsets = held.tile([P, N // 16], U16, name="offsets")
-        nc.sync.dma_start(offsets[:], offs)
+            if g == 0:
+                with nc.allow_non_contiguous_dma(reason="b1: GROUP float32 for each partition and group"):
+                    nc.sync.dma_start(b1_sb[:], b1.rearrange("(g p r) one -> p g (r one)", g=GB, r=GROUP))
         w2_sb = held.tile([P, GB, GROUP, C], BF16, name="w2_sb")
         nc.sync.dma_start(w2_sb[:], w2.rearrange("(g p r) c -> p g r c", g=GB, r=GROUP))
+        offsets = held.tile([P, N // 16], U16, name="offsets")
+        nc.sync.dma_start(offsets[:], offs)
         b2_sb = held.tile([P, CB], F32, name="b2_sb")
         with nc.allow_non_contiguous_dma(reason="b2: one float32 for each partition and channel block"):
-            nc.scalar.dma_start(b2_sb[:], b2.rearrange("(cb p) one -> p (cb one)", p=P))
+            nc.sync.dma_start(b2_sb[:], b2.rearrange("(cb p) one -> p (cb one)", p=P))
         table = [held.tile([P, S], F32, name=f"table{cb}") for cb in range(CB)]
         for cb in range(CB):
             nc.sync.dma_start(table[cb][:], atom_tab[cb * P : (cb + 1) * P, :])

@@ -71,23 +71,33 @@ def tile_cdvae_kernel(tc, atom_tab, t, tw, w1, b1, w2, b2, offs, out):
         quarter = held.tile([P, 1], F32, name="quarter")
         nc.vector.memset(quarter[:], 0.5 * math.pi)
         e = [held.tile([P, N], BF16, name=f"e{kb}") for kb in range(KB)]
-        turns = [banks.tile([P, HALF], F32, name="turns", tag="bank") for half in halves]
+        cuts = [[slice(0, PIECE), slice(PIECE, HALF)], [halves[1]]]
+        turns = [[banks.tile([P, cut.stop - cut.start], F32, name="turns", tag="bank") for cut in cuts[h]] for h in range(len(halves))]
+        for h, half in enumerate(halves):
+            for cut, turns_cut in zip(cuts[h], turns[h]):
+                nc.tensor.matmul(
+                    turns_cut[:], tw_pad[:], t_pad[h][:, cut.start - half.start : cut.stop - half.start], start=True, stop=True
+                )
         for h in range(len(halves)):
-            nc.tensor.matmul(turns[h][:], tw_pad[:], t_pad[h][:], start=True, stop=True)
-        for half, turns_half in zip(halves, turns):
-            nc.scalar.activation(e[0][:, half], turns_half[:], FUNC.Sin, scale=2.0 * math.pi)
-            nc.scalar.activation(e[1][:, half], turns_half[:], FUNC.Sin, bias=quarter[:], scale=2.0 * math.pi)
+            for cut, turns_cut in zip(cuts[h], turns[h]):
+                nc.scalar.activation(e[0][:, cut], turns_cut[:], FUNC.Sin, scale=2.0 * math.pi)
+                nc.scalar.activation(e[1][:, cut], turns_cut[:], FUNC.Sin, bias=quarter[:], scale=2.0 * math.pi)
 
         u = [[held.tile([P, N], BF16, name=f"u{g}_{r}") for r in range(GROUP)] for g in range(GB)]
         w1_blocks = [[w1_sb[kb][g][:].rearrange("k (p r) -> k r p", r=GROUP) for g in range(GB)] for kb in range(KB)]
-        for half in halves:
+        for h, half in enumerate(halves):
             for g in range(GB):
                 v = [banks.tile([P, HALF], F32, name="v", tag="bank") for r in range(GROUP)]
-                for kb in range(KB):
-                    for r in range(GROUP):
-                        nc.tensor.matmul(
-                            v[r][:], w1_blocks[kb][g][:, r, :], e[kb][:, half], start=kb == 0, stop=kb == KB - 1
-                        )
+                for cut in cuts[h] if g == 0 else [half]:
+                    for kb in range(KB):
+                        for r in range(GROUP):
+                            nc.tensor.matmul(
+                                v[r][:, cut.start - half.start : cut.stop - half.start],
+                                w1_blocks[kb][g][:, r, :],
+                                e[kb][:, cut],
+                                start=kb == 0,
+                                stop=kb == KB - 1,
+                            )
                 for r in range(GROUP):
                     nc.scalar.activation(u[g][r][:, half], v[r][:], FUNC.Silu, bias=b1_sb[:, g, r : r + 1])
 

import math

import concourse.mybir as mybir

F32 = mybir.dt.float32
BF16 = mybir.dt.bfloat16
U16 = mybir.dt.uint16
FUNC = mybir.ActivationFunctionType
ADD = mybir.AluOpType.add

P = 128
C, F, S, N = 256, 1024, 1024, 512
KB = C // P
FB = F // P
CB = C // P
PIECE = 128
SMALL = 64
HALF = N // 2
GROUP = 4
GB = FB // GROUP
WARM = 12

FLOPS = 2 * N * (C * F + F * C)


def tile_cdvae_kernel(tc, atom_tab, t, tw, w1, b1, w2, b2, offs, out):
    nc = tc.nc
    with (
        tc.tile_pool(name="held", bufs=1) as held,
        tc.psum_pool(name="banks", bufs=8) as banks,
    ):
        idle = held.tile([P, P], BF16, name="idle")
        tw_pad = held.tile([P, P], F32, name="tw_pad")
        nc.gpsimd.memset(tw_pad[:], 0.0)
        nc.gpsimd.memset(idle[:], 0.0)
        spin = banks.tile([P, P], F32, name="spin", tag="bank")
        for rep in range(WARM):
            nc.tensor.matmul(spin[:], idle[:], idle[:], start=True, stop=True)

        halves = [slice(first, first + HALF) for first in range(0, N, HALF)]

        nc.sync.dma_start(tw_pad[0:1, :], tw.rearrange("k one -> one k"))
        t_pad = [held.tile([P, HALF], F32, name=f"t_pad{h}") for h in range(len(halves))]
        for h, half in enumerate(halves):
            nc.vector.memset(t_pad[h][:], 0.0)
            nc.sync.dma_start(t_pad[h][0:1, :], t[:, half])
        w1_sb = [[held.tile([P, GROUP * P], BF16, name=f"w1_{kb}_{g}") for g in range(GB)] for kb in range(KB)]
        b1_sb = held.tile([P, GB, GROUP], F32, name="b1_sb")
        for g in range(GB):
            for kb in range(KB):
                nc.sync.dma_start(w1_sb[kb][g][:], w1[kb * P : (kb + 1) * P, g * GROUP * P : (g + 1) * GROUP * P])
            if g == 0:
                with nc.allow_non_contiguous_dma(reason="b1: GROUP float32 for each partition and group"):
                    nc.sync.dma_start(b1_sb[:], b1.rearrange("(g p r) one -> p g (r one)", g=GB, r=GROUP))
        w2_sb = held.tile([P, GB, GROUP, C], BF16, name="w2_sb")
        nc.sync.dma_start(w2_sb[:], w2.rearrange("(g p r) c -> p g r c", g=GB, r=GROUP))
        offsets = held.tile([P, N // 16], U16, name="offsets")
        nc.sync.dma_start(offsets[:], offs)
        b2_sb = held.tile([P, CB], F32, name="b2_sb")
        with nc.allow_non_contiguous_dma(reason="b2: one float32 for each partition and channel block"):
            nc.sync.dma_start(b2_sb[:], b2.rearrange("(cb p) one -> p (cb one)", p=P))
        table = [held.tile([P, S], F32, name=f"table{cb}") for cb in range(CB)]
        for cb in range(CB):
            nc.sync.dma_start(table[cb][:], atom_tab[cb * P : (cb + 1) * P, :])

        zero = held.tile([P, 1], F32, name="zero")
        nc.vector.memset(zero[:], 0.0)
        primed = held.tile([P, 1], F32, name="primed")
        nc.scalar.activation(primed[:], zero[:], FUNC.Silu)

        quarter = held.tile([P, 1], F32, name="quarter")
        nc.vector.memset(quarter[:], 0.5 * math.pi)
        e = [held.tile([P, N], BF16, name=f"e{kb}") for kb in range(KB)]
        cuts = [[slice(0, PIECE), slice(PIECE, HALF)], [halves[1]]]
        turns = [[banks.tile([P, cut.stop - cut.start], F32, name="turns", tag="bank") for cut in cuts[h]] for h in range(len(halves))]
        for h, half in enumerate(halves):
            for cut, turns_cut in zip(cuts[h], turns[h]):
                nc.tensor.matmul(
                    turns_cut[:], tw_pad[:], t_pad[h][:, cut.start - half.start : cut.stop - half.start], start=True, stop=True
                )
        for h in range(len(halves)):
            for cut, turns_cut in zip(cuts[h], turns[h]):
                nc.scalar.activation(e[0][:, cut], turns_cut[:], FUNC.Sin, scale=2.0 * math.pi)
                nc.scalar.activation(e[1][:, cut], turns_cut[:], FUNC.Sin, bias=quarter[:], scale=2.0 * math.pi)

        u = [[held.tile([P, N], BF16, name=f"u{g}_{r}") for r in range(GROUP)] for g in range(GB)]
        w1_blocks = [[w1_sb[kb][g][:].rearrange("k (p r) -> k r p", r=GROUP) for g in range(GB)] for kb in range(KB)]
        for h, half in enumerate(halves):
            for g in range(GB):
                v = [banks.tile([P, HALF], F32, name="v", tag="bank") for r in range(GROUP)]
                for cut in cuts[h] if g == 0 else [half]:
                    for kb in range(KB):
                        for r in range(GROUP):
                            nc.tensor.matmul(
                                v[r][:, cut.start - half.start : cut.stop - half.start],
                                w1_blocks[kb][g][:, r, :],
                                e[kb][:, cut],
                                start=kb == 0,
                                stop=kb == KB - 1,
                            )
                for r in range(GROUP):
                    nc.scalar.activation(u[g][r][:, half], v[r][:], FUNC.Silu, bias=b1_sb[:, g, r : r + 1])

        te = [held.tile([P, N], F32, name=f"te{cb}") for cb in range(CB)]
        res = [held.tile([P, N], F32, name=f"res{cb}") for cb in range(CB)]
        for half in halves:
            for cb in range(CB):
                last = half == halves[-1] and cb == CB - 1
                step = SMALL if last else PIECE
                for first in range(half.start, half.stop, step):
                    piece = slice(first, first + step)
                    acc = banks.tile([P, step], F32, name="acc", tag="bank")
                    for fb in range(FB):
                        g, r = divmod(fb, GROUP)
                        nc.tensor.matmul(
                            acc[:], w2_sb[:, g, r, cb * P : (cb + 1) * P], u[g][r][:, piece], start=fb == 0, stop=fb == FB - 1
                        )
                    nc.scalar.activation(te[cb][:, piece], acc[:], FUNC.Identity, bias=b2_sb[:, cb : cb + 1])
                    picked = table[cb][:].indirect(offsets[:, first // 16 : (first + step) // 16])
                    nc.vector.tensor_tensor(res[cb][:, piece], picked, te[cb][:, piece], ADD)
                    nc.sync.dma_start(out[cb * P : (cb + 1) * P, piece], res[cb][:, piece])
